import numpy as np
import ml_dtypes


def mxq(x, axis, fmt="e4m3"):
    dtype, down = {"e4m3": (ml_dtypes.float8_e4m3fn, 7), "e5m2": (ml_dtypes.float8_e5m2, 14)}[fmt]
    v = np.moveaxis(np.asarray(x, np.float32).astype(ml_dtypes.bfloat16).astype(np.float64), axis, -1)
    blocks = v.reshape(v.shape[:-1] + (-1, 32))
    amax = np.abs(blocks).max(-1, keepdims=True)
    byte = np.maximum(np.where(amax > 0, np.frexp(amax)[1] - 1 + 127, 0) - down, 1)
    scale = np.exp2(byte - 127.0)
    codes = (blocks / scale).astype(np.float32).astype(dtype).astype(np.float64)
    return np.moveaxis((codes * scale).reshape(v.shape), -1, axis)


WIDE = False


def mx_kscale(k):
    if not WIDE:
        return np.ones(k)
    levels = np.array([10, -10, 5, -5, 0])
    a = np.random.permutation(np.resize(levels, k // 512 * 4)).reshape(k // 512, 4)
    idx = np.arange(k)
    return np.exp2(a[idx // 512, idx % 128 // 32])


BF16 = ml_dtypes.bfloat16


def bf(x):
    return np.asarray(x, np.float32).astype(BF16)


def f64(x):
    return np.asarray(x).astype(np.float64)


B, IN, OUT, POOL_K = 512, 2048, 4096, 4
SCALE = 2.0


def _gelu_tanh(p):
    return 0.5 * p * (1.0 + np.tanh(0.7978845608 * (p + 0.044715 * p * p * p)))


def setup_inputs():
    s = mx_kscale(IN)
    return {"x": bf(np.random.standard_normal((B, IN)) * s),
            "weight": bf(np.random.standard_normal((OUT, IN)) * (1.0 / np.sqrt(IN)) / s[None, :]),
            "bias": bf(np.random.standard_normal(OUT) * 0.5)}


def reference(x, weight, bias):
    rows = x.shape[0]
    width = weight.shape[0]
    y = (mxq(f64(x), 1, "e4m3") @ mxq(f64(weight), 1, "e4m3").T) + f64(bias)
    pooled = y.reshape(rows, width // POOL_K, POOL_K).mean(axis=-1)
    scaled = _gelu_tanh(pooled) * SCALE
    return np.max(scaled, axis=1)

@@ -1,0 +1,163 @@
+from contextlib import ExitStack
+
+import concourse.mybir as mybir
+from concourse.masks import make_identity
+
+F32 = mybir.dt.float32
+BF16 = mybir.dt.bfloat16
+U32 = mybir.dt.uint32
+U8 = mybir.dt.uint8
+FP8X4 = mybir.dt.float8_e4m3fn_x4
+ACT = mybir.ActivationFunctionType
+ALU = mybir.AluOpType
+AX = mybir.AxisListType
+
+P = 128
+B, K, OUT, POOL_K = 512, 2048, 4096, 4
+FLOPS = 2 * B * K * OUT
+PASSES = K // 512
+J_TILES = OUT // POOL_K // P
+UNITS = 2 * J_TILES
+W_EVAC = ("S", "S", "V", "S")
+X_EVAC = ("S", "V", "S", "V")
+
+
+def tile_modelnew_kernel(tc, x, weight, bias, out):
+    nc = tc.nc
+    with ExitStack() as ctx:
+        keep = ctx.enter_context(tc.tile_pool(name="keep", bufs=1))
+        stage = ctx.enter_context(tc.tile_pool(name="stage", bufs=3))
+        epi = ctx.enter_context(tc.tile_pool(name="epi", bufs=2))
+        psum_t = ctx.enter_context(tc.psum_pool(name="psum_t", bufs=6))
+        psum_acc = ctx.enter_context(tc.psum_pool(name="psum_acc", bufs=2))
+        ctx.enter_context(tc.manual_schedule())
+
+        bias_raw = keep.tile([P, J_TILES, POOL_K], BF16)
+        nc.scalar.dma_start(out=bias_raw[:], in_=bias.rearrange("(t p i) -> p t i", p=P, i=POOL_K))
+        x_view = x.rearrange("(c p) k -> c p k", p=P)
+        x_raw = []
+        for c in range(4):
+            xr = keep.tile([P, K], BF16, name="x_raw%d" % c)
+            nc.sync.dma_start(out=xr[:], in_=x_view[c])
+            x_raw.append(xr)
+        w_view = weight.rearrange("(t p i) k -> t p (i k)", p=P, i=POOL_K)
+        w_raw = []
+        for n in range(UNITS):
+            wr = keep.tile([P, 2 * K], BF16, name="w_raw%d" % n)
+            half = n % 2
+            nc.sync.dma_start(out=wr[:], in_=w_view[n // 2][:, half * 2 * K : (half + 1) * 2 * K])
+            w_raw.append(wr)
+
+        ident = keep.tile([P, P], F32)
+        make_identity(nc, ident[:])
+        warm = keep.tile([P, 1], F32)
+        nc.vector.memset(warm[:], 0.0)
+        res = keep.tile([P, 32], F32, align_bytes=64)
+        nc.vector.memset(res[:], 0.0)
+        warm_out = keep.tile([P, 1], F32)
+        nc.scalar.activation(out=warm_out[:], in_=warm[:], func=ACT.Gelu_apprx_tanh)
+        bias_sum = keep.tile([P, J_TILES], F32)
+        nc.vector.tensor_reduce(out=bias_sum[:], in_=bias_raw[:], axis=AX.X, op=ALU.add)
+        bias_p = keep.tile([P, J_TILES], F32)
+        nc.vector.tensor_scalar_mul(out=bias_p[:], in0=bias_sum[:], scalar1=1.0 / POOL_K)
+
+        def transpose_bank(sources):
+            bank = psum_t.tile([P, 4, P], F32, tag="bank")
+            for q in range(4):
+                nc.tensor.transpose(bank[:, q, :], sources[q], ident[:])
+            return bank
+
+        def evacuate(engine, words, bank):
+            dst = words.rearrange("p (h j u) -> p h j u", h=2, u=2)
+            src = bank[:].rearrange("p (h u) j -> p h j u", u=2)
+            if engine == "S":
+                nc.scalar.copy(out=dst, in_=src)
+            else:
+                nc.vector.tensor_copy(out=dst, in_=src)
+
+        x_grouped = keep.tile([P, 4 * K], BF16, align_bytes=64)
+        x_words = x_grouped[:].bitcast(F32)
+        x_codes = keep.tile([P, PASSES * B], U32, align_bytes=64)
+        x_scales = keep.tile([P, PASSES * B], U8, align_bytes=64)
+        for cp in range(2):
+            banks = []
+            for g in range(PASSES):
+                srcs = []
+                for cl in range(2):
+                    xw = x_raw[2 * cp + cl][:].bitcast(F32)
+                    for u in range(2):
+                        off = g * 256 + u * P
+                        srcs.append(xw[:, off : off + P])
+                banks.append(transpose_bank(srcs))
+            for g in range(PASSES):
+                off = g * 1024 + cp * 512
+                evacuate(X_EVAC[g], x_words[:, off : off + 512], banks[g])
+        for g in range(PASSES):
+            nc.vector.quantize_mx(
+                out=x_codes[:, g * B : (g + 1) * B].bitcast(FP8X4),
+                scales=x_scales[:, g * B : (g + 1) * B],
+                in_=x_grouped[:, g * 4 * B : (g + 1) * 4 * B],
+            )
+
+        best = keep.tile([P, B], F32)
+        state = {}
+
+        def multiply(n):
+            if n % 2 == 0:
+                state["acc"] = psum_acc.tile([P, B], F32, tag="acc", name="acc")
+            acc = state["acc"]
+            codes, scales = state[n]
+            for o in range(8):
+                g = o % PASSES
+                nc.tensor.matmul_mx(
+                    out=acc[:],
+                    lhsT=codes[:, o * P : (o + 1) * P].bitcast(FP8X4),
+                    lhsT_scale=scales[:, o * P : (o + 1) * P],
+                    rhs=x_codes[:, g * B : (g + 1) * B].bitcast(FP8X4),
+                    rhs_scale=x_scales[:, g * B : (g + 1) * B],
+                    start=(n % 2 == 0 and o == 0),
+                    stop=(n % 2 == 1 and o == 7),
+                )
+
+        def epilogue(t):
+            acc = state["acc"]
+            act = epi.tile([P, B], F32, tag="act", name="act")
+            nc.scalar.activation(
+                out=act[:], in_=acc[:], func=ACT.Gelu_apprx_tanh, bias=bias_p[:, t : t + 1], scale=1.0 / POOL_K
+            )
+            if t == 0:
+                nc.vector.tensor_scalar_mul(out=best[:], in0=act[:], scalar1=2.0)
+            else:
+                nc.vector.scalar_tensor_tensor(
+                    out=best[:], in0=act[:], scalar=2.0, in1=best[:], op0=ALU.mult, op1=ALU.max
+                )
+
+        for n in range(UNITS + 1):
+            if n < UNITS:
+                ww = w_raw[n][:].bitcast(F32)
+                banks = [
+                    transpose_bank([ww[:, (4 * b + q) * P : (4 * b + q + 1) * P] for q in range(4)]) for b in range(4)
+                ]
+                grouped = stage.tile([P, 4 * K // 2], BF16, tag="grouped", name="grouped", align_bytes=64)
+                gwords = grouped[:].bitcast(F32)
+                for b in range(4):
+                    evacuate(W_EVAC[b], gwords[:, b * 512 : (b + 1) * 512], banks[b])
+            if n > 0:
+                multiply(n - 1)
+            if n < UNITS:
+                codes = stage.tile([P, 8 * P], U32, tag="codes", name="codes", align_bytes=64)
+                scales = stage.tile([P, 8 * P], U8, tag="scales", name="scales", align_bytes=64)
+                nc.vector.quantize_mx(out=codes[:].bitcast(FP8X4), scales=scales[:], in_=grouped[:])
+                state[n] = (codes, scales)
+            if n > 0 and n % 2 == 0:
+                epilogue(n // 2 - 1)
+
+        fin = psum_t.tile([P, 4, P], F32, tag="bank", name="fin")
+        for q in range(4):
+            nc.tensor.transpose(fin[:, q, :], best[:, q * P : (q + 1) * P], ident[:])
+        nc.vector.tensor_reduce(out=res[:, 0:4], in_=fin[:], axis=AX.X, op=ALU.max)
+        res_t = keep.tile([P, 32], F32, align_bytes=64)
+        nc.vector.transpose(out=res_t[:], in_=res[:])
+        out_view = out.rearrange("(c a r) -> c a r", a=4, r=32)
+        for c in range(4):
+            nc.sync.dma_start(out=out_view[c], in_=res_t[c : P : 32, :])

@@ -132,25 +132,37 @@ def tile_modelnew_kernel(tc, x, weight, bias, out):
                     out=best[:], in0=act[:], scalar=2.0, in1=best[:], op0=ALU.mult, op1=ALU.max
                 )
 
-        for n in range(UNITS + 1):
-            if n < UNITS:
-                ww = w_raw[n][:].bitcast(F32)
-                banks = [
-                    transpose_bank([ww[:, (4 * b + q) * P : (4 * b + q + 1) * P] for q in range(4)]) for b in range(4)
-                ]
-                grouped = stage.tile([P, 4 * K // 2], BF16, tag="grouped", name="grouped", align_bytes=64)
-                gwords = grouped[:].bitcast(F32)
-                for b in range(4):
-                    evacuate(W_EVAC[b], gwords[:, b * 512 : (b + 1) * 512], banks[b])
-            if n > 0:
-                multiply(n - 1)
-            if n < UNITS:
-                codes = stage.tile([P, 8 * P], U32, tag="codes", name="codes", align_bytes=64)
-                scales = stage.tile([P, 8 * P], U8, tag="scales", name="scales", align_bytes=64)
-                nc.vector.quantize_mx(out=codes[:].bitcast(FP8X4), scales=scales[:], in_=grouped[:])
-                state[n] = (codes, scales)
-            if n > 0 and n % 2 == 0:
-                epilogue(n // 2 - 1)
+        def transpose_unit(n):
+            ww = w_raw[n][:].bitcast(F32)
+            return [transpose_bank([ww[:, (4 * b + q) * P : (4 * b + q + 1) * P] for q in range(4)]) for b in range(4)]
+
+        def evacuate_unit(n, banks):
+            grouped = stage.tile([P, 2 * K], BF16, tag="grouped", name="grouped", align_bytes=64)
+            gwords = grouped[:].bitcast(F32)
+            for b in range(4):
+                evacuate(W_EVAC[b], gwords[:, b * 512 : (b + 1) * 512], banks[b])
+            return grouped
+
+        def quantise_unit(n, grouped):
+            codes = stage.tile([P, 8 * P], U32, tag="codes", name="codes", align_bytes=64)
+            scales = stage.tile([P, 8 * P], U8, tag="scales", name="scales", align_bytes=64)
+            nc.vector.quantize_mx(out=codes[:].bitcast(FP8X4), scales=scales[:], in_=grouped[:])
+            state[n] = (codes, scales)
+
+        for t in range(J_TILES):
+            banks_a = transpose_unit(2 * t)
+            banks_b = transpose_unit(2 * t + 1)
+            grouped_a = evacuate_unit(2 * t, banks_a)
+            quantise_unit(2 * t, grouped_a)
+            grouped_b = evacuate_unit(2 * t + 1, banks_b)
+            if t > 0:
+                multiply(2 * t - 1)
+            quantise_unit(2 * t + 1, grouped_b)
+            if t > 0:
+                epilogue(t - 1)
+            multiply(2 * t)
+        multiply(UNITS - 1)
+        epilogue(J_TILES - 1)
 
         fin = psum_t.tile([P, 4, P], F32, tag="bank", name="fin")
         for q in range(4):

@@ -19,7 +19,7 @@ PASSES = K // 512
 J_TILES = OUT // POOL_K // P
 UNITS = 2 * J_TILES
 W_EVAC = ("S", "S", "V", "S")
-X_EVAC = ("S", "V", "S", "V")
+HALF = B // 2
 
 
 def tile_modelnew_kernel(tc, x, weight, bias, out):
@@ -33,14 +33,14 @@ def tile_modelnew_kernel(tc, x, weight, bias, out):
         ctx.enter_context(tc.manual_schedule())
 
         bias_raw = keep.tile([P, J_TILES, POOL_K], BF16)
-        nc.scalar.dma_start(out=bias_raw[:], in_=bias.rearrange("(t p i) -> p t i", p=P, i=POOL_K))
+        nc.scalar.dma_start(out=bias_raw[:], in_=bias.rearrange("(p t i) -> p t i", t=J_TILES, i=POOL_K))
         x_view = x.rearrange("(c p) k -> c p k", p=P)
         x_raw = []
         for c in range(4):
             xr = keep.tile([P, K], BF16, name="x_raw%d" % c)
             nc.sync.dma_start(out=xr[:], in_=x_view[c])
             x_raw.append(xr)
-        w_view = weight.rearrange("(t p i) k -> t p (i k)", p=P, i=POOL_K)
+        w_view = weight.rearrange("(p t i) k -> t p (i k)", t=J_TILES, i=POOL_K)
         w_raw = []
         for n in range(UNITS):
             wr = keep.tile([P, 2 * K], BF16, name="w_raw%d" % n)
@@ -61,14 +61,13 @@ def tile_modelnew_kernel(tc, x, weight, bias, out):
         bias_p = keep.tile([P, J_TILES], F32)
         nc.vector.tensor_scalar_mul(out=bias_p[:], in0=bias_sum[:], scalar1=1.0 / POOL_K)
 
-        def transpose_bank(sources):
+        def transpose_bank(words, first):
             bank = psum_t.tile([P, 4, P], F32, tag="bank")
             for q in range(4):
-                nc.tensor.transpose(bank[:, q, :], sources[q], ident[:])
+                nc.tensor.transpose(bank[:, q, :], words[:, (first + q) * P : (first + q + 1) * P], ident[:])
             return bank
 
-        def evacuate(engine, words, bank):
-            dst = words.rearrange("p (h j u) -> p h j u", h=2, u=2)
+        def evacuate(engine, dst, bank):
             src = bank[:].rearrange("p (h u) j -> p h j u", u=2)
             if engine == "S":
                 nc.scalar.copy(out=dst, in_=src)
@@ -76,98 +75,106 @@ def tile_modelnew_kernel(tc, x, weight, bias, out):
                 nc.vector.tensor_copy(out=dst, in_=src)
 
         x_grouped = keep.tile([P, 4 * K], BF16, align_bytes=64)
-        x_words = x_grouped[:].bitcast(F32)
+        x_words = x_grouped[:].bitcast(F32).rearrange("p (g c w) -> p g c w", g=PASSES, c=4)
         x_codes = keep.tile([P, PASSES * B], U32, align_bytes=64)
         x_scales = keep.tile([P, PASSES * B], U8, align_bytes=64)
-        for cp in range(2):
-            banks = []
+        for c in range(4):
+            xw = x_raw[c][:].bitcast(F32)
+            banks = [transpose_bank(xw, 4 * gh) for gh in range(2)]
+            for gh in range(2):
+                dst = x_words[:, 2 * gh : 2 * gh + 2, c, :].rearrange("p h (j u) -> p h j u", u=2)
+                evacuate("SV"[gh], dst, banks[gh])
             for g in range(PASSES):
-                srcs = []
-                for cl in range(2):
-                    xw = x_raw[2 * cp + cl][:].bitcast(F32)
-                    for u in range(2):
-                        off = g * 256 + u * P
-                        srcs.append(xw[:, off : off + P])
-                banks.append(transpose_bank(srcs))
-            for g in range(PASSES):
-                off = g * 1024 + cp * 512
-                evacuate(X_EVAC[g], x_words[:, off : off + 512], banks[g])
-        for g in range(PASSES):
-            nc.vector.quantize_mx(
-                out=x_codes[:, g * B : (g + 1) * B].bitcast(FP8X4),
-                scales=x_scales[:, g * B : (g + 1) * B],
-                in_=x_grouped[:, g * 4 * B : (g + 1) * 4 * B],
-            )
+                lo = g * B + c * P
+                nc.vector.quantize_mx(
+                    out=x_codes[:, lo : lo + P].bitcast(FP8X4),
+                    scales=x_scales[:, lo : lo + P],
+                    in_=x_grouped[:, 4 * lo : 4 * (lo + P)],
+                )
 
         best = keep.tile([P, B], F32)
-        state = {}
+        quantised = {}
 
-        def multiply(n):
-            if n % 2 == 0:
-                state["acc"] = psum_acc.tile([P, B], F32, tag="acc", name="acc")
-            acc = state["acc"]
-            codes, scales = state[n]
+        def multiply(n, acc, lo, width):
+            codes, scales = quantised[n]
             for o in range(8):
-                g = o % PASSES
+                first = (o % PASSES) * B + lo
                 nc.tensor.matmul_mx(
                     out=acc[:],
                     lhsT=codes[:, o * P : (o + 1) * P].bitcast(FP8X4),
                     lhsT_scale=scales[:, o * P : (o + 1) * P],
-                    rhs=x_codes[:, g * B : (g + 1) * B].bitcast(FP8X4),
-                    rhs_scale=x_scales[:, g * B : (g + 1) * B],
+                    rhs=x_codes[:, first : first + width].bitcast(FP8X4),
+                    rhs_scale=x_scales[:, first : first + width],
                     start=(n % 2 == 0 and o == 0),
                     stop=(n % 2 == 1 and o == 7),
                 )
 
-        def epilogue(t):
-            acc = state["acc"]
-            act = epi.tile([P, B], F32, tag="act", name="act")
+        def gelu(t, acc, width):
+            act = epi.tile([P, width], F32, tag="act", name="act")
             nc.scalar.activation(
                 out=act[:], in_=acc[:], func=ACT.Gelu_apprx_tanh, bias=bias_p[:, t : t + 1], scale=1.0 / POOL_K
             )
-            if t == 0:
-                nc.vector.tensor_scalar_mul(out=best[:], in0=act[:], scalar1=2.0)
-            else:
-                nc.vector.scalar_tensor_tensor(
-                    out=best[:], in0=act[:], scalar=2.0, in1=best[:], op0=ALU.mult, op1=ALU.max
-                )
+            return act
+
+        def keep_larger(running, act):
+            nc.vector.scalar_tensor_tensor(out=running, in0=act, scalar=2.0, in1=running, op0=ALU.mult, op1=ALU.max)
 
         def transpose_unit(n):
             ww = w_raw[n][:].bitcast(F32)
-            return [transpose_bank([ww[:, (4 * b + q) * P : (4 * b + q + 1) * P] for q in range(4)]) for b in range(4)]
+            return [transpose_bank(ww, 4 * b) for b in range(4)]
 
-        def evacuate_unit(n, banks):
+        def evacuate_unit(banks):
             grouped = stage.tile([P, 2 * K], BF16, tag="grouped", name="grouped", align_bytes=64)
             gwords = grouped[:].bitcast(F32)
             for b in range(4):
-                evacuate(W_EVAC[b], gwords[:, b * 512 : (b + 1) * 512], banks[b])
+                dst = gwords[:, b * 512 : (b + 1) * 512].rearrange("p (h j u) -> p h j u", h=2, u=2)
+                evacuate(W_EVAC[b], dst, banks[b])
             return grouped
 
         def quantise_unit(n, grouped):
             codes = stage.tile([P, 8 * P], U32, tag="codes", name="codes", align_bytes=64)
             scales = stage.tile([P, 8 * P], U8, tag="scales", name="scales", align_bytes=64)
             nc.vector.quantize_mx(out=codes[:].bitcast(FP8X4), scales=scales[:], in_=grouped[:])
-            state[n] = (codes, scales)
+            quantised[n] = (codes, scales)
 
+        acc = None
         for t in range(J_TILES):
             banks_a = transpose_unit(2 * t)
             banks_b = transpose_unit(2 * t + 1)
-            grouped_a = evacuate_unit(2 * t, banks_a)
+            grouped_a = evacuate_unit(banks_a)
             quantise_unit(2 * t, grouped_a)
-            grouped_b = evacuate_unit(2 * t + 1, banks_b)
+            grouped_b = evacuate_unit(banks_b)
             if t > 0:
-                multiply(2 * t - 1)
+                multiply(2 * t - 1, acc, 0, B)
             quantise_unit(2 * t + 1, grouped_b)
             if t > 0:
-                epilogue(t - 1)
-            multiply(2 * t)
-        multiply(UNITS - 1)
-        epilogue(J_TILES - 1)
+                act = gelu(t - 1, acc, B)
+                if t == 1:
+                    nc.vector.tensor_scalar_mul(out=best[:], in0=act[:], scalar1=2.0)
+                else:
+                    keep_larger(best[:], act[:])
+            if t < J_TILES - 1:
+                acc = psum_acc.tile([P, B], F32, tag="acc", name="acc")
+                multiply(2 * t, acc, 0, B)
 
-        fin = psum_t.tile([P, 4, P], F32, tag="bank", name="fin")
-        for q in range(4):
-            nc.tensor.transpose(fin[:, q, :], best[:, q * P : (q + 1) * P], ident[:])
+        last = J_TILES - 1
+        acc_a = psum_acc.tile([P, HALF], F32, tag="acc", name="acc_a")
+        multiply(UNITS - 2, acc_a, 0, HALF)
+        multiply(UNITS - 1, acc_a, 0, HALF)
+        act_a = gelu(last, acc_a, HALF)
+        keep_larger(best[:, 0:HALF], act_a[:])
+        acc_b = psum_acc.tile([P, HALF], F32, tag="acc", name="acc_b")
+        multiply(UNITS - 2, acc_b, HALF, HALF)
+        multiply(UNITS - 1, acc_b, HALF, HALF)
+        fin = transpose_bank(best[:], 0)
+        act_b = gelu(last, acc_b, HALF)
         nc.vector.tensor_reduce(out=res[:, 0:4], in_=fin[:], axis=AX.X, op=ALU.max)
+        fin_b = psum_t.tile([P, 4, P], F32, tag="bank", name="fin_b")
+        for q in range(2):
+            nc.tensor.transpose(fin_b[:, q, :], act_b[:, q * P : (q + 1) * P], ident[:])
+        res_b = keep.tile([P, 2], F32)
+        nc.vector.tensor_reduce(out=res_b[:], in_=fin_b[:, 0:2, :], axis=AX.X, op=ALU.max)
+        keep_larger(res[:, 2:4], res_b[:])
         res_t = keep.tile([P, 32], F32, align_bytes=64)
         nc.vector.transpose(out=res_t[:], in_=res[:])
         out_view = out.rearrange("(c a r) -> c a r", a=4, r=32)

@@ -20,6 +20,7 @@ J_TILES = OUT // POOL_K // P
 UNITS = 2 * J_TILES
 W_EVAC = ("S", "S", "V", "S")
 HALF = B // 2
+X_IDLE = (4, 2, 2, 2)
 
 
 def tile_modelnew_kernel(tc, x, weight, bias, out):
@@ -48,6 +49,8 @@ def tile_modelnew_kernel(tc, x, weight, bias, out):
             nc.sync.dma_start(out=wr[:], in_=w_view[n // 2][:, half * 2 * K : (half + 1) * 2 * K])
             w_raw.append(wr)
 
+        idle_in = keep.tile([P, B], BF16)
+        nc.vector.memset(idle_in[:], 0.0)
         ident = keep.tile([P, P], F32)
         make_identity(nc, ident[:])
         warm = keep.tile([P, 1], F32)
@@ -60,6 +63,12 @@ def tile_modelnew_kernel(tc, x, weight, bias, out):
         nc.vector.tensor_reduce(out=bias_sum[:], in_=bias_raw[:], axis=AX.X, op=ALU.add)
         bias_p = keep.tile([P, J_TILES], F32)
         nc.vector.tensor_scalar_mul(out=bias_p[:], in0=bias_sum[:], scalar1=1.0 / POOL_K)
+
+        idle_out = psum_acc.tile([P, B], F32, tag="acc", name="idle_out")
+
+        def keep_busy(count):
+            for unused in range(count):
+                nc.tensor.matmul(out=idle_out[:], lhsT=idle_in[:, 0:P], rhs=idle_in[:], start=True, stop=True)
 
         def transpose_bank(words, first):
             bank = psum_t.tile([P, 4, P], F32, tag="bank")
@@ -79,6 +88,7 @@ def tile_modelnew_kernel(tc, x, weight, bias, out):
         x_codes = keep.tile([P, PASSES * B], U32, align_bytes=64)
         x_scales = keep.tile([P, PASSES * B], U8, align_bytes=64)
         for c in range(4):
+            keep_busy(X_IDLE[c])
             xw = x_raw[c][:].bitcast(F32)
             banks = [transpose_bank(xw, 4 * gh) for gh in range(2)]
             for gh in range(2):
@@ -139,7 +149,11 @@ def tile_modelnew_kernel(tc, x, weight, bias, out):
 
         acc = None
         for t in range(J_TILES):
+            if t == 0:
+                keep_busy(4)
             banks_a = transpose_unit(2 * t)
+            if t == 0:
+                keep_busy(3)
             banks_b = transpose_unit(2 * t + 1)
             grouped_a = evacuate_unit(banks_a)
             quantise_unit(2 * t, grouped_a)

@@ -20,6 +20,8 @@ J_TILES = OUT // POOL_K // P
 UNITS = 2 * J_TILES
 W_EVAC = ("S", "S", "V", "S")
 HALF = B // 2
+W_BUFS = 9
+GROUPS = ((0, 1), (2, 3), (4, 5, 6, 7), (8, 9, 10, 11), (12, 13, 14, 15))
 X_IDLE = (4, 2, 2, 2)
 
 
@@ -27,7 +29,9 @@ def tile_modelnew_kernel(tc, x, weight, bias, out):
     nc = tc.nc
     with ExitStack() as ctx:
         keep = ctx.enter_context(tc.tile_pool(name="keep", bufs=1))
-        stage = ctx.enter_context(tc.tile_pool(name="stage", bufs=3))
+        loads = ctx.enter_context(tc.tile_pool(name="loads", bufs=W_BUFS))
+        stage = ctx.enter_context(tc.tile_pool(name="stage", bufs=4))
+        coded = ctx.enter_context(tc.tile_pool(name="coded", bufs=6))
         epi = ctx.enter_context(tc.tile_pool(name="epi", bufs=2))
         psum_t = ctx.enter_context(tc.psum_pool(name="psum_t", bufs=6))
         psum_acc = ctx.enter_context(tc.psum_pool(name="psum_acc", bufs=2))
@@ -43,11 +47,17 @@ def tile_modelnew_kernel(tc, x, weight, bias, out):
             x_raw.append(xr)
         w_view = weight.rearrange("(p t i) k -> t p (i k)", t=J_TILES, i=POOL_K)
         w_raw = []
-        for n in range(UNITS):
-            wr = keep.tile([P, 2 * K], BF16, name="w_raw%d" % n)
-            half = n % 2
-            nc.sync.dma_start(out=wr[:], in_=w_view[n // 2][:, half * 2 * K : (half + 1) * 2 * K])
-            w_raw.append(wr)
+
+        def load_unit():
+            n = len(w_raw)
+            if n < UNITS:
+                wr = loads.tile([P, 2 * K], BF16, tag="w_raw", name="w_raw")
+                half = n % 2
+                nc.sync.dma_start(out=wr[:], in_=w_view[n // 2][:, half * 2 * K : (half + 1) * 2 * K])
+                w_raw.append(wr)
+
+        for n in range(W_BUFS):
+            load_unit()
 
         idle_in = keep.tile([P, B], BF16)
         nc.vector.memset(idle_in[:], 0.0)
@@ -131,45 +141,69 @@ def tile_modelnew_kernel(tc, x, weight, bias, out):
 
         def transpose_unit(n):
             ww = w_raw[n][:].bitcast(F32)
-            return [transpose_bank(ww, 4 * b) for b in range(4)]
+            banks = [transpose_bank(ww, 4 * b) for b in range(4)]
+            load_unit()
+            return banks
 
-        def evacuate_unit(banks):
+        def evacuate_unit(banks, engines):
             grouped = stage.tile([P, 2 * K], BF16, tag="grouped", name="grouped", align_bytes=64)
             gwords = grouped[:].bitcast(F32)
             for b in range(4):
                 dst = gwords[:, b * 512 : (b + 1) * 512].rearrange("p (h j u) -> p h j u", h=2, u=2)
-                evacuate(W_EVAC[b], dst, banks[b])
+                evacuate(engines[b], dst, banks[b])
             return grouped
 
         def quantise_unit(n, grouped):
-            codes = stage.tile([P, 8 * P], U32, tag="codes", name="codes", align_bytes=64)
-            scales = stage.tile([P, 8 * P], U8, tag="scales", name="scales", align_bytes=64)
+            codes = coded.tile([P, 8 * P], U32, tag="codes", name="codes", align_bytes=64)
+            scales = coded.tile([P, 8 * P], U8, tag="scales", name="scales", align_bytes=64)
             nc.vector.quantize_mx(out=codes[:].bitcast(FP8X4), scales=scales[:], in_=grouped[:])
             quantised[n] = (codes, scales)
 
-        acc = None
-        for t in range(J_TILES):
+        accs = {}
+
+        def multiply_unit(n):
+            if n % 2 == 0:
+                accs[n // 2] = psum_acc.tile([P, B], F32, tag="acc", name="acc")
+            multiply(n, accs[n // 2], 0, B)
+
+        def finish_tile(t):
+            act = gelu(t, accs[t], B)
             if t == 0:
-                keep_busy(4)
-            banks_a = transpose_unit(2 * t)
-            if t == 0:
-                keep_busy(3)
-            banks_b = transpose_unit(2 * t + 1)
-            grouped_a = evacuate_unit(banks_a)
-            quantise_unit(2 * t, grouped_a)
-            grouped_b = evacuate_unit(banks_b)
-            if t > 0:
-                multiply(2 * t - 1, acc, 0, B)
-            quantise_unit(2 * t + 1, grouped_b)
-            if t > 0:
-                act = gelu(t - 1, acc, B)
-                if t == 1:
-                    nc.vector.tensor_scalar_mul(out=best[:], in0=act[:], scalar1=2.0)
-                else:
-                    keep_larger(best[:], act[:])
-            if t < J_TILES - 1:
-                acc = psum_acc.tile([P, B], F32, tag="acc", name="acc")
-                multiply(2 * t, acc, 0, B)
+                nc.vector.tensor_scalar_mul(out=best[:], in0=act[:], scalar1=2.0)
+            else:
+                keep_larger(best[:], act[:])
+
+        for group in GROUPS:
+            first = group[0]
+            banks = []
+            for n in group:
+                if n == 0:
+                    keep_busy(4)
+                if n == 1:
+                    keep_busy(3)
+                banks.append(transpose_unit(n))
+            if len(group) == 2:
+                grouped_a = evacuate_unit(banks[0], W_EVAC)
+                quantise_unit(first, grouped_a)
+                grouped_b = evacuate_unit(banks[1], W_EVAC)
+                if first > 0:
+                    multiply_unit(first - 1)
+                quantise_unit(first + 1, grouped_b)
+                if first > 0:
+                    finish_tile(first // 2 - 1)
+                multiply_unit(first)
+            else:
+                grouped = [evacuate_unit(banks[i], "SVSV") for i in range(4)]
+                multiply_unit(first - 1)
+                for i in range(3):
+                    quantise_unit(first + i, grouped[i])
+                finish_tile(first // 2 - 1)
+                multiply_unit(first)
+                multiply_unit(first + 1)
+                quantise_unit(first + 3, grouped[3])
+                finish_tile(first // 2)
+                if first + 2 < UNITS - 2:
+                    multiply_unit(first + 2)
 
         last = J_TILES - 1
         acc_a = psum_acc.tile([P, HALF], F32, tag="acc", name="acc_a")

@@ -21,7 +21,7 @@ UNITS = 2 * J_TILES
 W_EVAC = ("S", "S", "V", "S")
 HALF = B // 2
 W_BUFS = 9
-GROUPS = ((0, 1), (2, 3), (4, 5, 6, 7), (8, 9, 10, 11), (12, 13, 14, 15))
+GROUPS = ((0, 1), (2, 3), (4, 5, 6, 7), (8, 9, 10, 11, 12, 13, 14, 15))
 X_IDLE = (4, 2, 2, 2)
 
 
@@ -30,7 +30,7 @@ def tile_modelnew_kernel(tc, x, weight, bias, out):
     with ExitStack() as ctx:
         keep = ctx.enter_context(tc.tile_pool(name="keep", bufs=1))
         loads = ctx.enter_context(tc.tile_pool(name="loads", bufs=W_BUFS))
-        stage = ctx.enter_context(tc.tile_pool(name="stage", bufs=4))
+        stage = ctx.enter_context(tc.tile_pool(name="stage", bufs=8))
         coded = ctx.enter_context(tc.tile_pool(name="coded", bufs=6))
         epi = ctx.enter_context(tc.tile_pool(name="epi", bufs=2))
         psum_t = ctx.enter_context(tc.psum_pool(name="psum_t", bufs=6))
@@ -193,17 +193,19 @@ def tile_modelnew_kernel(tc, x, weight, bias, out):
                     finish_tile(first // 2 - 1)
                 multiply_unit(first)
             else:
-                grouped = [evacuate_unit(banks[i], "SVSV") for i in range(4)]
+                grouped = [evacuate_unit(b, "SVSV") for b in banks]
                 multiply_unit(first - 1)
-                for i in range(3):
+                quantise_unit(first, grouped[0])
+                quantise_unit(first + 1, grouped[1])
+                for i in range(2, len(group), 2):
                     quantise_unit(first + i, grouped[i])
-                finish_tile(first // 2 - 1)
-                multiply_unit(first)
-                multiply_unit(first + 1)
-                quantise_unit(first + 3, grouped[3])
-                finish_tile(first // 2)
-                if first + 2 < UNITS - 2:
-                    multiply_unit(first + 2)
+                    finish_tile((first + i) // 2 - 2)
+                    multiply_unit(first + i - 2)
+                    multiply_unit(first + i - 1)
+                    quantise_unit(first + i + 1, grouped[i + 1])
+                finish_tile(group[-1] // 2 - 1)
+                if group[-1] < UNITS - 1:
+                    multiply_unit(group[-1] - 1)
 
         last = J_TILES - 1
         acc_a = psum_acc.tile([P, HALF], F32, tag="acc", name="acc_a")

@@ -21,7 +21,7 @@ UNITS = 2 * J_TILES
 W_EVAC = ("S", "S", "V", "S")
 HALF = B // 2
 W_BUFS = 9
-GROUPS = ((0, 1), (2, 3), (4, 5, 6, 7), (8, 9, 10, 11, 12, 13, 14, 15))
+GROUPS = ((4, 5, 6, 7), (8, 9, 10, 11, 12, 13, 14, 15))
 X_IDLE = (4, 2, 2, 2)
 
 
@@ -41,10 +41,13 @@ def tile_modelnew_kernel(tc, x, weight, bias, out):
         nc.scalar.dma_start(out=bias_raw[:], in_=bias.rearrange("(p t i) -> p t i", t=J_TILES, i=POOL_K))
         x_view = x.rearrange("(c p) k -> c p k", p=P)
         x_raw = []
-        for c in range(4):
+
+        def load_x():
+            c = len(x_raw)
             xr = keep.tile([P, K], BF16, name="x_raw%d" % c)
             nc.sync.dma_start(out=xr[:], in_=x_view[c])
             x_raw.append(xr)
+
         w_view = weight.rearrange("(p t i) k -> t p (i k)", t=J_TILES, i=POOL_K)
         w_raw = []
 
@@ -56,7 +59,12 @@ def tile_modelnew_kernel(tc, x, weight, bias, out):
                 nc.sync.dma_start(out=wr[:], in_=w_view[n // 2][:, half * 2 * K : (half + 1) * 2 * K])
                 w_raw.append(wr)
 
-        for n in range(W_BUFS):
+        load_x()
+        load_x()
+        load_unit()
+        load_x()
+        load_x()
+        for n in range(1, W_BUFS):
             load_unit()
 
         idle_in = keep.tile([P, B], BF16)
@@ -97,7 +105,8 @@ def tile_modelnew_kernel(tc, x, weight, bias, out):
         x_words = x_grouped[:].bitcast(F32).rearrange("p (g c w) -> p g c w", g=PASSES, c=4)
         x_codes = keep.tile([P, PASSES * B], U32, align_bytes=64)
         x_scales = keep.tile([P, PASSES * B], U8, align_bytes=64)
-        for c in range(4):
+
+        def turn_x(c):
             keep_busy(X_IDLE[c])
             xw = x_raw[c][:].bitcast(F32)
             banks = [transpose_bank(xw, 4 * gh) for gh in range(2)]
@@ -161,6 +170,31 @@ def tile_modelnew_kernel(tc, x, weight, bias, out):
 
         accs = {}
 
+        def halves():
+            return [psum_acc.tile([P, HALF], F32, tag="acc", name="acc_half%d" % h) for h in range(2)]
+
+        turn_x(0)
+        turn_x(1)
+        keep_busy(2)
+        banks = transpose_unit(0)
+        quantise_unit(0, evacuate_unit(banks, W_EVAC))
+        turn_x(2)
+        turn_x(3)
+        acc_halves = halves()
+        multiply(0, acc_halves[0], 0, HALF)
+        banks = transpose_unit(1)
+        quantise_unit(1, evacuate_unit(banks, W_EVAC))
+        multiply(0, acc_halves[1], HALF, HALF)
+        banks = [transpose_unit(2), transpose_unit(3)]
+        quantise_unit(2, evacuate_unit(banks[0], W_EVAC))
+        grouped_b = evacuate_unit(banks[1], W_EVAC)
+        multiply(1, acc_halves[0], 0, HALF)
+        multiply(1, acc_halves[1], HALF, HALF)
+        quantise_unit(3, grouped_b)
+        for h in range(2):
+            act = gelu(0, acc_halves[h], HALF)
+            nc.vector.tensor_scalar_mul(out=best[:, h * HALF : (h + 1) * HALF], in0=act[:], scalar1=2.0)
+
         def multiply_unit(n):
             if n % 2 == 0:
                 accs[n // 2] = psum_acc.tile([P, B], F32, tag="acc", name="acc")
@@ -168,44 +202,26 @@ def tile_modelnew_kernel(tc, x, weight, bias, out):
 
         def finish_tile(t):
             act = gelu(t, accs[t], B)
-            if t == 0:
-                nc.vector.tensor_scalar_mul(out=best[:], in0=act[:], scalar1=2.0)
-            else:
-                keep_larger(best[:], act[:])
+            keep_larger(best[:], act[:])
+
+        multiply_unit(2)
 
         for group in GROUPS:
             first = group[0]
-            banks = []
-            for n in group:
-                if n == 0:
-                    keep_busy(4)
-                if n == 1:
-                    keep_busy(3)
-                banks.append(transpose_unit(n))
-            if len(group) == 2:
-                grouped_a = evacuate_unit(banks[0], W_EVAC)
-                quantise_unit(first, grouped_a)
-                grouped_b = evacuate_unit(banks[1], W_EVAC)
-                if first > 0:
-                    multiply_unit(first - 1)
-                quantise_unit(first + 1, grouped_b)
-                if first > 0:
-                    finish_tile(first // 2 - 1)
-                multiply_unit(first)
-            else:
-                grouped = [evacuate_unit(b, "SVSV") for b in banks]
-                multiply_unit(first - 1)
-                quantise_unit(first, grouped[0])
-                quantise_unit(first + 1, grouped[1])
-                for i in range(2, len(group), 2):
-                    quantise_unit(first + i, grouped[i])
-                    finish_tile((first + i) // 2 - 2)
-                    multiply_unit(first + i - 2)
-                    multiply_unit(first + i - 1)
-                    quantise_unit(first + i + 1, grouped[i + 1])
-                finish_tile(group[-1] // 2 - 1)
-                if group[-1] < UNITS - 1:
-                    multiply_unit(group[-1] - 1)
+            banks = [transpose_unit(n) for n in group]
+            grouped = [evacuate_unit(b, "SVSV") for b in banks]
+            multiply_unit(first - 1)
+            quantise_unit(first, grouped[0])
+            quantise_unit(first + 1, grouped[1])
+            for i in range(2, len(group), 2):
+                quantise_unit(first + i, grouped[i])
+                finish_tile((first + i) // 2 - 2)
+                multiply_unit(first + i - 2)
+                multiply_unit(first + i - 1)
+                quantise_unit(first + i + 1, grouped[i + 1])
+            finish_tile(group[-1] // 2 - 1)
+            if group[-1] < UNITS - 1:
+                multiply_unit(group[-1] - 1)
 
         last = J_TILES - 1
         acc_a = psum_acc.tile([P, HALF], F32, tag="acc", name="acc_a")

@@ -6,6 +6,7 @@ from concourse.masks import make_identity
 F32 = mybir.dt.float32
 BF16 = mybir.dt.bfloat16
 U32 = mybir.dt.uint32
+I32 = mybir.dt.int32
 U8 = mybir.dt.uint8
 FP8X4 = mybir.dt.float8_e4m3fn_x4
 ACT = mybir.ActivationFunctionType
@@ -18,10 +19,14 @@ FLOPS = 2 * B * K * OUT
 PASSES = K // 512
 J_TILES = OUT // POOL_K // P
 UNITS = 2 * J_TILES
+LAST = UNITS - 1
+QUADS = 4
+XW = B + 64 + B // 4
+X_SCALE = 4 * B + 128
 W_EVAC = ("S", "S", "V", "S")
 HALF = B // 2
-W_BUFS = 9
-GROUPS = ((4, 5, 6, 7), (8, 9, 10, 11, 12, 13, 14, 15))
+W_BUFS = 7
+GROUPS = ((4, 5, 6, 7), (8, 9, 10, 11, 12, 13, 14))
 X_IDLE = (4, 2, 2, 2)
 
 
@@ -30,8 +35,9 @@ def tile_modelnew_kernel(tc, x, weight, bias, out):
     with ExitStack() as ctx:
         keep = ctx.enter_context(tc.tile_pool(name="keep", bufs=1))
         loads = ctx.enter_context(tc.tile_pool(name="loads", bufs=W_BUFS))
-        stage = ctx.enter_context(tc.tile_pool(name="stage", bufs=8))
+        stage = ctx.enter_context(tc.tile_pool(name="stage", bufs=7))
         coded = ctx.enter_context(tc.tile_pool(name="coded", bufs=6))
+        turned = ctx.enter_context(tc.tile_pool(name="turned", bufs=2))
         epi = ctx.enter_context(tc.tile_pool(name="epi", bufs=2))
         psum_t = ctx.enter_context(tc.psum_pool(name="psum_t", bufs=6))
         psum_acc = ctx.enter_context(tc.psum_pool(name="psum_acc", bufs=2))
@@ -50,10 +56,17 @@ def tile_modelnew_kernel(tc, x, weight, bias, out):
 
         w_view = weight.rearrange("(p t i) k -> t p (i k)", t=J_TILES, i=POOL_K)
         w_raw = []
+        q_view = weight.rearrange("(s r t i) (q w) -> t i q r s w", s=QUADS, r=32, t=J_TILES, i=POOL_K, q=QUADS)
+        q_raw = keep.tile([P, 2, QUADS, K // QUADS], BF16, align_bytes=64)
+
+        def load_quadrants():
+            for m in range(2):
+                for q in (0, 2, 1, 3):
+                    nc.sync.dma_start(out=q_raw[32 * q : 32 * q + 32, m], in_=q_view[J_TILES - 1][2 + m][q])
 
         def load_unit():
             n = len(w_raw)
-            if n < UNITS:
+            if n < LAST:
                 wr = loads.tile([P, 2 * K], BF16, tag="w_raw", name="w_raw")
                 half = n % 2
                 nc.sync.dma_start(out=wr[:], in_=w_view[n // 2][:, half * 2 * K : (half + 1) * 2 * K])
@@ -69,6 +82,9 @@ def tile_modelnew_kernel(tc, x, weight, bias, out):
 
         idle_in = keep.tile([P, B], BF16)
         nc.vector.memset(idle_in[:], 0.0)
+        xq = keep.tile([P, PASSES * XW], U32, align_bytes=256)
+        nc.gpsimd.memset(xq[:].rearrange("p (g w) -> p g w", g=PASSES)[:, :, B:XW], 0)
+        xd = keep.tile([P, PASSES * XW], U32, align_bytes=256)
         ident = keep.tile([P, P], F32)
         make_identity(nc, ident[:])
         warm = keep.tile([P, 1], F32)
@@ -103,8 +119,8 @@ def tile_modelnew_kernel(tc, x, weight, bias, out):
 
         x_grouped = keep.tile([P, 4 * K], BF16, align_bytes=64)
         x_words = x_grouped[:].bitcast(F32).rearrange("p (g c w) -> p g c w", g=PASSES, c=4)
-        x_codes = keep.tile([P, PASSES * B], U32, align_bytes=64)
-        x_scales = keep.tile([P, PASSES * B], U8, align_bytes=64)
+        xq8 = xq[:].bitcast(U8)
+        xd8 = xd[:].bitcast(U8)
 
         def turn_x(c):
             keep_busy(X_IDLE[c])
@@ -115,25 +131,37 @@ def tile_modelnew_kernel(tc, x, weight, bias, out):
                 evacuate("SV"[gh], dst, banks[gh])
             for g in range(PASSES):
                 lo = g * B + c * P
+                code = g * XW + c * P
+                scale = 4 * g * XW + X_SCALE + c * P
                 nc.vector.quantize_mx(
-                    out=x_codes[:, lo : lo + P].bitcast(FP8X4),
-                    scales=x_scales[:, lo : lo + P],
+                    out=xq[:, code : code + P].bitcast(FP8X4),
+                    scales=xq8[:, scale : scale + P],
                     in_=x_grouped[:, 4 * lo : 4 * (lo + P)],
                 )
+
+        def exchange_x():
+            for g in range(PASSES):
+                for q in (0, 2, 1, 3):
+                    nc.sync.dma_start(
+                        out=xd[32 * q : 32 * q + 32, g * XW : (g + 1) * XW].bitcast(I32),
+                        in_=xq[32 * g : 32 * g + 32, q * XW : (q + 1) * XW].bitcast(I32),
+                    )
 
         best = keep.tile([P, B], F32)
         quantised = {}
 
         def multiply(n, acc, lo, width):
             codes, scales = quantised[n]
+            operand, operand8 = (xd, xd8) if n == LAST else (xq, xq8)
             for o in range(8):
-                first = (o % PASSES) * B + lo
+                first = (o % PASSES) * XW + lo
+                first8 = 4 * (o % PASSES) * XW + X_SCALE + lo
                 nc.tensor.matmul_mx(
                     out=acc[:],
                     lhsT=codes[:, o * P : (o + 1) * P].bitcast(FP8X4),
                     lhsT_scale=scales[:, o * P : (o + 1) * P],
-                    rhs=x_codes[:, first : first + width].bitcast(FP8X4),
-                    rhs_scale=x_scales[:, first : first + width],
+                    rhs=operand[:, first : first + width].bitcast(FP8X4),
+                    rhs_scale=operand8[:, first8 : first8 + width],
                     start=(n % 2 == 0 and o == 0),
                     stop=(n % 2 == 1 and o == 7),
                 )
@@ -163,10 +191,25 @@ def tile_modelnew_kernel(tc, x, weight, bias, out):
             return grouped
 
         def quantise_unit(n, grouped):
-            codes = coded.tile([P, 8 * P], U32, tag="codes", name="codes", align_bytes=64)
-            scales = coded.tile([P, 8 * P], U8, tag="scales", name="scales", align_bytes=64)
-            nc.vector.quantize_mx(out=codes[:].bitcast(FP8X4), scales=scales[:], in_=grouped[:])
+            codes_padded = coded.tile([P, 16 + 8 * P], U32, tag="codes", name="codes", align_bytes=256)
+            scales_padded = coded.tile([P, 192 + 8 * P], U8, tag="scales", name="scales", align_bytes=256)
+            codes = codes_padded[:, 16 : 16 + 8 * P]
+            scales = scales_padded[:, 192 : 192 + 8 * P]
+            nc.vector.quantize_mx(out=codes.bitcast(FP8X4), scales=scales, in_=grouped[:])
             quantised[n] = (codes, scales)
+
+        def turn_member(m):
+            turned_words = turned.tile([P, K // 2], F32, tag="turned", name="turned_words", align_bytes=64)
+            nc.vector.transpose(
+                out=turned_words[:], in_=q_raw[:, m].rearrange("p s w -> p (s w)").bitcast(F32)
+            )
+            return turned_words
+
+        def group_member(m, turned_words, grouped):
+            gwords = grouped[:].bitcast(F32).rearrange("p (m g s r u) -> p m g s r u", m=2, g=PASSES, s=QUADS, u=2)
+            src = turned_words[:].rearrange("p (s u g r) -> p s g r u", s=QUADS, u=2, g=PASSES)
+            for s in range(QUADS):
+                nc.scalar.copy(out=gwords[:, m, :, s], in_=src[:, s])
 
         accs = {}
 
@@ -210,18 +253,42 @@ def tile_modelnew_kernel(tc, x, weight, bias, out):
             first = group[0]
             banks = [transpose_unit(n) for n in group]
             grouped = [evacuate_unit(b, "SVSV") for b in banks]
+            if first == 4:
+                load_quadrants()
+                exchange_x()
             multiply_unit(first - 1)
             quantise_unit(first, grouped[0])
             quantise_unit(first + 1, grouped[1])
-            for i in range(2, len(group), 2):
-                quantise_unit(first + i, grouped[i])
-                finish_tile((first + i) // 2 - 2)
-                multiply_unit(first + i - 2)
-                multiply_unit(first + i - 1)
-                quantise_unit(first + i + 1, grouped[i + 1])
-            finish_tile(group[-1] // 2 - 1)
-            if group[-1] < UNITS - 1:
-                multiply_unit(group[-1] - 1)
+            if first == 4:
+                quantise_unit(6, grouped[2])
+                finish_tile(1)
+                multiply_unit(4)
+                multiply_unit(5)
+                quantise_unit(7, grouped[3])
+                finish_tile(2)
+                multiply_unit(6)
+            else:
+                quantise_unit(10, grouped[2])
+                finish_tile(3)
+                multiply_unit(8)
+                multiply_unit(9)
+                quantise_unit(11, grouped[3])
+                last_grouped = stage.tile([P, 2 * K], BF16, tag="grouped", name="last_grouped", align_bytes=64)
+                turned_words = turn_member(0)
+                quantise_unit(12, grouped[4])
+                group_member(0, turned_words, last_grouped)
+                finish_tile(4)
+                multiply_unit(10)
+                multiply_unit(11)
+                turned_words = turn_member(1)
+                quantise_unit(13, grouped[5])
+                group_member(1, turned_words, last_grouped)
+                quantise_unit(14, grouped[6])
+                finish_tile(5)
+                multiply_unit(12)
+                multiply_unit(13)
+                quantise_unit(LAST, last_grouped)
+                finish_tile(6)
 
         last = J_TILES - 1
         acc_a = psum_acc.tile([P, HALF], F32, tag="acc", name="acc_a")

@@ -6,7 +6,6 @@ from concourse.masks import make_identity
 F32 = mybir.dt.float32
 BF16 = mybir.dt.bfloat16
 U32 = mybir.dt.uint32
-I32 = mybir.dt.int32
 U8 = mybir.dt.uint8
 FP8X4 = mybir.dt.float8_e4m3fn_x4
 ACT = mybir.ActivationFunctionType
@@ -21,8 +20,6 @@ J_TILES = OUT // POOL_K // P
 UNITS = 2 * J_TILES
 LAST = UNITS - 1
 QUADS = 4
-XW = B + 64 + B // 4
-X_SCALE = 4 * B + 128
 W_EVAC = ("S", "S", "V", "S")
 HALF = B // 2
 W_BUFS = 7
@@ -56,13 +53,16 @@ def tile_modelnew_kernel(tc, x, weight, bias, out):
 
         w_view = weight.rearrange("(p t i) k -> t p (i k)", t=J_TILES, i=POOL_K)
         w_raw = []
-        q_view = weight.rearrange("(s r t i) (q w) -> t i q r s w", s=QUADS, r=32, t=J_TILES, i=POOL_K, q=QUADS)
-        q_raw = keep.tile([P, 2, QUADS, K // QUADS], BF16, align_bytes=64)
+        q_view = weight.rearrange(
+            "(s r t i) (h q w) -> t i s q r h w", s=QUADS, r=32, t=J_TILES, i=POOL_K, q=QUADS, w=64
+        )
+        q_raw = keep.tile([P, 2, QUADS, 2 * PASSES, 64], BF16, align_bytes=64)
 
         def load_quadrants():
             for m in range(2):
-                for q in (0, 2, 1, 3):
-                    nc.sync.dma_start(out=q_raw[32 * q : 32 * q + 32, m], in_=q_view[J_TILES - 1][2 + m][q])
+                for s in range(QUADS):
+                    for q in (0, 2, 1, 3):
+                        nc.sync.dma_start(out=q_raw[32 * q : 32 * q + 32, m, s], in_=q_view[J_TILES - 1][2 + m][s][q])
 
         def load_unit():
             n = len(w_raw)
@@ -82,9 +82,6 @@ def tile_modelnew_kernel(tc, x, weight, bias, out):
 
         idle_in = keep.tile([P, B], BF16)
         nc.vector.memset(idle_in[:], 0.0)
-        xq = keep.tile([P, PASSES * XW], U32, align_bytes=256)
-        nc.gpsimd.memset(xq[:].rearrange("p (g w) -> p g w", g=PASSES)[:, :, B:XW], 0)
-        xd = keep.tile([P, PASSES * XW], U32, align_bytes=256)
         ident = keep.tile([P, P], F32)
         make_identity(nc, ident[:])
         warm = keep.tile([P, 1], F32)
@@ -119,8 +116,9 @@ def tile_modelnew_kernel(tc, x, weight, bias, out):
 
         x_grouped = keep.tile([P, 4 * K], BF16, align_bytes=64)
         x_words = x_grouped[:].bitcast(F32).rearrange("p (g c w) -> p g c w", g=PASSES, c=4)
-        xq8 = xq[:].bitcast(U8)
-        xd8 = xd[:].bitcast(U8)
+        x_codes = keep.tile([P, PASSES * B], U32, align_bytes=256)
+        x_scales_padded = keep.tile([P, 128 + PASSES * B], U8, align_bytes=256)
+        x_scales = x_scales_padded[:, 128 : 128 + PASSES * B]
 
         def turn_x(c):
             keep_busy(X_IDLE[c])
@@ -131,37 +129,25 @@ def tile_modelnew_kernel(tc, x, weight, bias, out):
                 evacuate("SV"[gh], dst, banks[gh])
             for g in range(PASSES):
                 lo = g * B + c * P
-                code = g * XW + c * P
-                scale = 4 * g * XW + X_SCALE + c * P
                 nc.vector.quantize_mx(
-                    out=xq[:, code : code + P].bitcast(FP8X4),
-                    scales=xq8[:, scale : scale + P],
+                    out=x_codes[:, lo : lo + P].bitcast(FP8X4),
+                    scales=x_scales[:, lo : lo + P],
                     in_=x_grouped[:, 4 * lo : 4 * (lo + P)],
                 )
-
-        def exchange_x():
-            for g in range(PASSES):
-                for q in (0, 2, 1, 3):
-                    nc.sync.dma_start(
-                        out=xd[32 * q : 32 * q + 32, g * XW : (g + 1) * XW].bitcast(I32),
-                        in_=xq[32 * g : 32 * g + 32, q * XW : (q + 1) * XW].bitcast(I32),
-                    )
 
         best = keep.tile([P, B], F32)
         quantised = {}
 
         def multiply(n, acc, lo, width):
             codes, scales = quantised[n]
-            operand, operand8 = (xd, xd8) if n == LAST else (xq, xq8)
             for o in range(8):
-                first = (o % PASSES) * XW + lo
-                first8 = 4 * (o % PASSES) * XW + X_SCALE + lo
+                first = (o % PASSES) * B + lo
                 nc.tensor.matmul_mx(
                     out=acc[:],
                     lhsT=codes[:, o * P : (o + 1) * P].bitcast(FP8X4),
                     lhsT_scale=scales[:, o * P : (o + 1) * P],
-                    rhs=operand[:, first : first + width].bitcast(FP8X4),
-                    rhs_scale=operand8[:, first8 : first8 + width],
+                    rhs=x_codes[:, first : first + width].bitcast(FP8X4),
+                    rhs_scale=x_scales[:, first : first + width],
                     start=(n % 2 == 0 and o == 0),
                     stop=(n % 2 == 1 and o == 7),
                 )
@@ -201,13 +187,13 @@ def tile_modelnew_kernel(tc, x, weight, bias, out):
         def turn_member(m):
             turned_words = turned.tile([P, K // 2], F32, tag="turned", name="turned_words", align_bytes=64)
             nc.vector.transpose(
-                out=turned_words[:], in_=q_raw[:, m].rearrange("p s w -> p (s w)").bitcast(F32)
+                out=turned_words[:], in_=q_raw[:, m].rearrange("p s h w -> p (s h w)").bitcast(F32)
             )
             return turned_words
 
         def group_member(m, turned_words, grouped):
             gwords = grouped[:].bitcast(F32).rearrange("p (m g s r u) -> p m g s r u", m=2, g=PASSES, s=QUADS, u=2)
-            src = turned_words[:].rearrange("p (s u g r) -> p s g r u", s=QUADS, u=2, g=PASSES)
+            src = turned_words[:].rearrange("p (s g u r) -> p s g r u", s=QUADS, u=2, g=PASSES)
             for s in range(QUADS):
                 nc.scalar.copy(out=gwords[:, m, :, s], in_=src[:, s])
 
@@ -255,7 +241,6 @@ def tile_modelnew_kernel(tc, x, weight, bias, out):
             grouped = [evacuate_unit(b, "SVSV") for b in banks]
             if first == 4:
                 load_quadrants()
-                exchange_x()
             multiply_unit(first - 1)
             quantise_unit(first, grouped[0])
             quantise_unit(first + 1, grouped[1])
@@ -273,18 +258,18 @@ def tile_modelnew_kernel(tc, x, weight, bias, out):
                 multiply_unit(8)
                 multiply_unit(9)
                 quantise_unit(11, grouped[3])
-                last_grouped = stage.tile([P, 2 * K], BF16, tag="grouped", name="last_grouped", align_bytes=64)
-                turned_words = turn_member(0)
                 quantise_unit(12, grouped[4])
-                group_member(0, turned_words, last_grouped)
                 finish_tile(4)
                 multiply_unit(10)
                 multiply_unit(11)
-                turned_words = turn_member(1)
                 quantise_unit(13, grouped[5])
-                group_member(1, turned_words, last_grouped)
+                last_grouped = stage.tile([P, 2 * K], BF16, tag="grouped", name="last_grouped", align_bytes=64)
+                turned_words = [turn_member(0)]
                 quantise_unit(14, grouped[6])
                 finish_tile(5)
+                turned_words.append(turn_member(1))
+                for m in range(2):
+                    group_member(m, turned_words[m], last_grouped)
                 multiply_unit(12)
                 multiply_unit(13)
                 quantise_unit(LAST, last_grouped)
@@ -292,13 +277,12 @@ def tile_modelnew_kernel(tc, x, weight, bias, out):
 
         last = J_TILES - 1
         acc_a = psum_acc.tile([P, HALF], F32, tag="acc", name="acc_a")
-        multiply(UNITS - 2, acc_a, 0, HALF)
-        multiply(UNITS - 1, acc_a, 0, HALF)
+        acc_b = psum_acc.tile([P, HALF], F32, tag="acc", name="acc_b")
+        for n in (UNITS - 2, UNITS - 1):
+            multiply(n, acc_a, 0, HALF)
+            multiply(n, acc_b, HALF, HALF)
         act_a = gelu(last, acc_a, HALF)
         keep_larger(best[:, 0:HALF], act_a[:])
-        acc_b = psum_acc.tile([P, HALF], F32, tag="acc", name="acc_b")
-        multiply(UNITS - 2, acc_b, HALF, HALF)
-        multiply(UNITS - 1, acc_b, HALF, HALF)
         fin = transpose_bank(best[:], 0)
         act_b = gelu(last, acc_b, HALF)
         nc.vector.tensor_reduce(out=res[:, 0:4], in_=fin[:], axis=AX.X, op=ALU.max)

from contextlib import ExitStack

import concourse.mybir as mybir
from concourse.masks import make_identity

F32 = mybir.dt.float32
BF16 = mybir.dt.bfloat16
U32 = mybir.dt.uint32
U8 = mybir.dt.uint8
FP8X4 = mybir.dt.float8_e4m3fn_x4
ACT = mybir.ActivationFunctionType
ALU = mybir.AluOpType
AX = mybir.AxisListType

P = 128
B, K, OUT, POOL_K = 512, 2048, 4096, 4
FLOPS = 2 * B * K * OUT
PASSES = K // 512
J_TILES = OUT // POOL_K // P
UNITS = 2 * J_TILES
LAST = UNITS - 1
QUADS = 4
W_EVAC = ("S", "S", "V", "S")
HALF = B // 2
W_BUFS = 7
GROUPS = ((4, 5, 6, 7), (8, 9, 10, 11, 12, 13, 14))
X_IDLE = (4, 2, 2, 2)


def tile_modelnew_kernel(tc, x, weight, bias, out):
    nc = tc.nc
    with ExitStack() as ctx:
        keep = ctx.enter_context(tc.tile_pool(name="keep", bufs=1))
        loads = ctx.enter_context(tc.tile_pool(name="loads", bufs=W_BUFS))
        stage = ctx.enter_context(tc.tile_pool(name="stage", bufs=7))
        coded = ctx.enter_context(tc.tile_pool(name="coded", bufs=6))
        turned = ctx.enter_context(tc.tile_pool(name="turned", bufs=2))
        epi = ctx.enter_context(tc.tile_pool(name="epi", bufs=2))
        psum_t = ctx.enter_context(tc.psum_pool(name="psum_t", bufs=6))
        psum_acc = ctx.enter_context(tc.psum_pool(name="psum_acc", bufs=2))
        ctx.enter_context(tc.manual_schedule())

        bias_raw = keep.tile([P, J_TILES, POOL_K], BF16)
        nc.scalar.dma_start(out=bias_raw[:], in_=bias.rearrange("(p t i) -> p t i", t=J_TILES, i=POOL_K))
        x_view = x.rearrange("(c p) k -> c p k", p=P)
        x_raw = []

        def load_x():
            c = len(x_raw)
            xr = keep.tile([P, K], BF16, name="x_raw%d" % c)
            nc.sync.dma_start(out=xr[:], in_=x_view[c])
            x_raw.append(xr)

        w_view = weight.rearrange("(p t i) k -> t p (i k)", t=J_TILES, i=POOL_K)
        w_raw = []
        q_view = weight.rearrange(
            "(s r t i) (h q w) -> t i s q r h w", s=QUADS, r=32, t=J_TILES, i=POOL_K, q=QUADS, w=64
        )
        q_raw = keep.tile([P, 2, QUADS, 2 * PASSES, 64], BF16, align_bytes=64)

        def load_quadrants():
            for m in range(2):
                for s in range(QUADS):
                    for q in (0, 2, 1, 3):
                        nc.sync.dma_start(out=q_raw[32 * q : 32 * q + 32, m, s], in_=q_view[J_TILES - 1][2 + m][s][q])

        def load_unit():
            n = len(w_raw)
            if n < LAST:
                wr = loads.tile([P, 2 * K], BF16, tag="w_raw", name="w_raw")
                half = n % 2
                nc.sync.dma_start(out=wr[:], in_=w_view[n // 2][:, half * 2 * K : (half + 1) * 2 * K])
                w_raw.append(wr)

        load_x()
        load_x()
        load_unit()
        load_x()
        load_x()
        for n in range(1, W_BUFS):
            load_unit()

        idle_in = keep.tile([P, B], BF16)
        nc.vector.memset(idle_in[:], 0.0)
        ident = keep.tile([P, P], F32)
        make_identity(nc, ident[:])
        warm = keep.tile([P, 1], F32)
        nc.vector.memset(warm[:], 0.0)
        res = keep.tile([P, 32], F32, align_bytes=64)
        nc.vector.memset(res[:], 0.0)
        warm_out = keep.tile([P, 1], F32)
        nc.scalar.activation(out=warm_out[:], in_=warm[:], func=ACT.Gelu_apprx_tanh)
        bias_sum = keep.tile([P, J_TILES], F32)
        nc.vector.tensor_reduce(out=bias_sum[:], in_=bias_raw[:], axis=AX.X, op=ALU.add)
        bias_p = keep.tile([P, J_TILES], F32)
        nc.vector.tensor_scalar_mul(out=bias_p[:], in0=bias_sum[:], scalar1=1.0 / POOL_K)

        idle_out = psum_acc.tile([P, B], F32, tag="acc", name="idle_out")

        def keep_busy(count):
            for unused in range(count):
                nc.tensor.matmul(out=idle_out[:], lhsT=idle_in[:, 0:P], rhs=idle_in[:], start=True, stop=True)

        def transpose_bank(words, first):
            bank = psum_t.tile([P, 4, P], F32, tag="bank")
            for q in range(4):
                nc.tensor.transpose(bank[:, q, :], words[:, (first + q) * P : (first + q + 1) * P], ident[:])
            return bank

        def evacuate(engine, dst, bank):
            src = bank[:].rearrange("p (h u) j -> p h j u", u=2)
            if engine == "S":
                nc.scalar.copy(out=dst, in_=src)
            else:
                nc.vector.tensor_copy(out=dst, in_=src)

        x_grouped = keep.tile([P, 4 * K], BF16, align_bytes=64)
        x_words = x_grouped[:].bitcast(F32).rearrange("p (g c w) -> p g c w", g=PASSES, c=4)
        x_codes = keep.tile([P, PASSES * B], U32, align_bytes=256)
        x_scales_padded = keep.tile([P, 128 + PASSES * B], U8, align_bytes=256)
        x_scales = x_scales_padded[:, 128 : 128 + PASSES * B]

        def turn_x(c):
            keep_busy(X_IDLE[c])
            xw = x_raw[c][:].bitcast(F32)
            banks = [transpose_bank(xw, 4 * gh) for gh in range(2)]
            for gh in range(2):
                dst = x_words[:, 2 * gh : 2 * gh + 2, c, :].rearrange("p h (j u) -> p h j u", u=2)
                evacuate("SV"[gh], dst, banks[gh])
            for g in range(PASSES):
                lo = g * B + c * P
                nc.vector.quantize_mx(
                    out=x_codes[:, lo : lo + P].bitcast(FP8X4),
                    scales=x_scales[:, lo : lo + P],
                    in_=x_grouped[:, 4 * lo : 4 * (lo + P)],
                )

        best = keep.tile([P, B], F32)
        quantised = {}

        def multiply(n, acc, lo, width):
            codes, scales = quantised[n]
            for o in range(8):
                first = (o % PASSES) * B + lo
                nc.tensor.matmul_mx(
                    out=acc[:],
                    lhsT=codes[:, o * P : (o + 1) * P].bitcast(FP8X4),
                    lhsT_scale=scales[:, o * P : (o + 1) * P],
                    rhs=x_codes[:, first : first + width].bitcast(FP8X4),
                    rhs_scale=x_scales[:, first : first + width],
                    start=(n % 2 == 0 and o == 0),
                    stop=(n % 2 == 1 and o == 7),
                )

        def gelu(t, acc, width):
            act = epi.tile([P, width], F32, tag="act", name="act")
            nc.scalar.activation(
                out=act[:], in_=acc[:], func=ACT.Gelu_apprx_tanh, bias=bias_p[:, t : t + 1], scale=1.0 / POOL_K
            )
            return act

        def keep_larger(running, act):
            nc.vector.scalar_tensor_tensor(out=running, in0=act, scalar=2.0, in1=running, op0=ALU.mult, op1=ALU.max)

        def transpose_unit(n):
            ww = w_raw[n][:].bitcast(F32)
            banks = [transpose_bank(ww, 4 * b) for b in range(4)]
            load_unit()
            return banks

        def evacuate_unit(banks, engines):
            grouped = stage.tile([P, 2 * K], BF16, tag="grouped", name="grouped", align_bytes=64)
            gwords = grouped[:].bitcast(F32)
            for b in range(4):
                dst = gwords[:, b * 512 : (b + 1) * 512].rearrange("p (h j u) -> p h j u", h=2, u=2)
                evacuate(engines[b], dst, banks[b])
            return grouped

        def quantise_unit(n, grouped):
            codes_padded = coded.tile([P, 16 + 8 * P], U32, tag="codes", name="codes", align_bytes=256)
            scales_padded = coded.tile([P, 192 + 8 * P], U8, tag="scales", name="scales", align_bytes=256)
            codes = codes_padded[:, 16 : 16 + 8 * P]
            scales = scales_padded[:, 192 : 192 + 8 * P]
            nc.vector.quantize_mx(out=codes.bitcast(FP8X4), scales=scales, in_=grouped[:])
            quantised[n] = (codes, scales)

        def turn_member(m):
            turned_words = turned.tile([P, K // 2], F32, tag="turned", name="turned_words", align_bytes=64)
            nc.vector.transpose(
                out=turned_words[:], in_=q_raw[:, m].rearrange("p s h w -> p (s h w)").bitcast(F32)
            )
            return turned_words

        def group_member(m, turned_words, grouped):
            gwords = grouped[:].bitcast(F32).rearrange("p (m g s r u) -> p m g s r u", m=2, g=PASSES, s=QUADS, u=2)
            src = turned_words[:].rearrange("p (s g u r) -> p s g r u", s=QUADS, u=2, g=PASSES)
            for s in range(QUADS):
                nc.scalar.copy(out=gwords[:, m, :, s], in_=src[:, s])

        accs = {}

        def halves():
            return [psum_acc.tile([P, HALF], F32, tag="acc", name="acc_half%d" % h) for h in range(2)]

        turn_x(0)
        turn_x(1)
        keep_busy(2)
        banks = transpose_unit(0)
        quantise_unit(0, evacuate_unit(banks, W_EVAC))
        turn_x(2)
        turn_x(3)
        acc_halves = halves()
        multiply(0, acc_halves[0], 0, HALF)
        banks = transpose_unit(1)
        quantise_unit(1, evacuate_unit(banks, W_EVAC))
        multiply(0, acc_halves[1], HALF, HALF)
        banks = [transpose_unit(2), transpose_unit(3)]
        quantise_unit(2, evacuate_unit(banks[0], W_EVAC))
        grouped_b = evacuate_unit(banks[1], W_EVAC)
        multiply(1, acc_halves[0], 0, HALF)
        multiply(1, acc_halves[1], HALF, HALF)
        quantise_unit(3, grouped_b)
        for h in range(2):
            act = gelu(0, acc_halves[h], HALF)
            nc.vector.tensor_scalar_mul(out=best[:, h * HALF : (h + 1) * HALF], in0=act[:], scalar1=2.0)

        def multiply_unit(n):
            if n % 2 == 0:
                accs[n // 2] = psum_acc.tile([P, B], F32, tag="acc", name="acc")
            multiply(n, accs[n // 2], 0, B)

        def finish_tile(t):
            act = gelu(t, accs[t], B)
            keep_larger(best[:], act[:])

        multiply_unit(2)

        for group in GROUPS:
            first = group[0]
            banks = [transpose_unit(n) for n in group]
            grouped = [evacuate_unit(b, "SVSV") for b in banks]
            if first == 4:
                load_quadrants()
            multiply_unit(first - 1)
            quantise_unit(first, grouped[0])
            quantise_unit(first + 1, grouped[1])
            if first == 4:
                quantise_unit(6, grouped[2])
                finish_tile(1)
                multiply_unit(4)
                multiply_unit(5)
                quantise_unit(7, grouped[3])
                finish_tile(2)
                multiply_unit(6)
            else:
                quantise_unit(10, grouped[2])
                finish_tile(3)
                multiply_unit(8)
                multiply_unit(9)
                quantise_unit(11, grouped[3])
                quantise_unit(12, grouped[4])
                finish_tile(4)
                multiply_unit(10)
                multiply_unit(11)
                quantise_unit(13, grouped[5])
                last_grouped = stage.tile([P, 2 * K], BF16, tag="grouped", name="last_grouped", align_bytes=64)
                turned_words = [turn_member(0)]
                quantise_unit(14, grouped[6])
                finish_tile(5)
                turned_words.append(turn_member(1))
                for m in range(2):
                    group_member(m, turned_words[m], last_grouped)
                multiply_unit(12)
                multiply_unit(13)
                quantise_unit(LAST, last_grouped)
                finish_tile(6)

        last = J_TILES - 1
        acc_a = psum_acc.tile([P, HALF], F32, tag="acc", name="acc_a")
        acc_b = psum_acc.tile([P, HALF], F32, tag="acc", name="acc_b")
        for n in (UNITS - 2, UNITS - 1):
            multiply(n, acc_a, 0, HALF)
            multiply(n, acc_b, HALF, HALF)
        act_a = gelu(last, acc_a, HALF)
        keep_larger(best[:, 0:HALF], act_a[:])
        fin = transpose_bank(best[:], 0)
        act_b = gelu(last, acc_b, HALF)
        nc.vector.tensor_reduce(out=res[:, 0:4], in_=fin[:], axis=AX.X, op=ALU.max)
        fin_b = psum_t.tile([P, 4, P], F32, tag="bank", name="fin_b")
        for q in range(2):
            nc.tensor.transpose(fin_b[:, q, :], act_b[:, q * P : (q + 1) * P], ident[:])
        res_b = keep.tile([P, 2], F32)
        nc.vector.tensor_reduce(out=res_b[:], in_=fin_b[:, 0:2, :], axis=AX.X, op=ALU.max)
        keep_larger(res[:, 2:4], res_b[:])
        res_t = keep.tile([P, 32], F32, align_bytes=64)
        nc.vector.transpose(out=res_t[:], in_=res[:])
        out_view = out.rearrange("(c a r) -> c a r", a=4, r=32)
        for c in range(4):
            nc.sync.dma_start(out=out_view[c], in_=res_t[c : P : 32, :])
